import numpy as np
import ml_dtypes

BF16 = ml_dtypes.bfloat16


def bf(x):
    return np.asarray(x, np.float32).astype(BF16)


def f32(x):
    return np.asarray(x, np.float32)


def f64(x):
    return np.asarray(x).astype(np.float64)


def striped(idx):
    return np.tile(idx.reshape(-1, 16).T, (8, 1))


T, H, M, S, N = 4, 128, 256, 1024, 2048


def setup_inputs():
    return {"x": f32(np.random.standard_normal((T * H, S))), "dst": f32(np.random.standard_normal((T * H, N))), "w_src": bf(np.random.standard_normal((H, M)) / np.sqrt(H)), "w_dst": bf(np.random.standard_normal((H, M)) / np.sqrt(H)), "b": f32(0.1 * np.random.standard_normal((M, 1))), "offs": striped(np.random.permutation(np.tile(np.arange(S), 2))[:N])}


def reference(x, dst, w_src, w_dst, b, offs):
    idx = offs[:16].T.reshape(-1)
    p = np.einsum("hm,thn->tmn", f64(w_src), f64(x).reshape(T, H, S))
    q = np.einsum("hm,thn->tmn", f64(w_dst), f64(dst).reshape(T, H, N)) + f64(b)[None]
    return (p[:, :, idx] + q).reshape(T * M, N)

@@ -1,0 +1,89 @@
+import concourse.mybir as mybir
+
+F32 = mybir.dt.float32
+BF16 = mybir.dt.bfloat16
+U16 = mybir.dt.uint16
+ADD = mybir.AluOpType.add
+IDENTITY = mybir.ActivationFunctionType.Identity
+COPY = mybir.ActivationFunctionType.Copy
+
+T = 4
+H = 128
+M = 256
+S = 1024
+N = 2048
+BANK = 512
+PIECE = 1024
+
+FLOPS = 2 * T * H * M * (S + N)
+
+
+def tile_globallocalencoder_kernel(tc, x, dst, w_src, w_dst, b, offs, out):
+    nc = tc.nc
+    with (
+        tc.tile_pool(name="held", bufs=1) as held,
+        tc.tile_pool(name="raw", bufs=T) as raw,
+        tc.tile_pool(name="rounded", bufs=2) as rounded,
+        tc.tile_pool(name="windows", bufs=3) as windows,
+        tc.tile_pool(name="pieces", bufs=4) as pieces,
+        tc.psum_pool(name="banks", bufs=4) as banks,
+    ):
+        offsets = held.tile([128, N // 16], U16, name="offsets")
+        nc.sync.dma_start(offsets[:], offs)
+
+        w_src_sb = held.tile([H, M], BF16, name="w_src_sb")
+        w_dst_sb = held.tile([H, M], BF16, name="w_dst_sb")
+        nc.scalar.dma_start(w_src_sb[:], w_src)
+        nc.scalar.dma_start(w_dst_sb[:], w_dst)
+        bias = [held.tile([128, 1], F32, name=f"bias{g}") for g in range(M // 128)]
+        for g in range(M // 128):
+            nc.scalar.dma_start(bias[g][:], b[g * 128 : (g + 1) * 128, :])
+
+        x_raw = []
+        dst_raw = []
+        for t in range(T):
+            x_t = raw.tile([H, S], F32, name="x_t")
+            nc.sync.dma_start(x_t[:], x[t * H : (t + 1) * H, :])
+            d_t = raw.tile([H, N], F32, name="d_t")
+            for c in range(N // PIECE):
+                cols = slice(c * PIECE, (c + 1) * PIECE)
+                nc.sync.dma_start(d_t[:, cols], dst[t * H : (t + 1) * H, cols])
+            x_raw.append(x_t)
+            dst_raw.append(d_t)
+
+        for t in range(T):
+            x_bf = rounded.tile([H, S], BF16, name="x_bf")
+            nc.gpsimd.tensor_copy(x_bf[:], x_raw[t][:])
+            d_bf = rounded.tile([H, N], BF16, name="d_bf")
+            for c in range(N // PIECE):
+                cols = slice(c * PIECE, (c + 1) * PIECE)
+                nc.gpsimd.tensor_copy(d_bf[:, cols], dst_raw[t][:, cols])
+
+            for g in range(M // 128):
+                rows = slice(g * 128, (g + 1) * 128)
+                window = windows.tile([128, S], F32, name="window")
+                for c in range(S // BANK):
+                    cols = slice(c * BANK, (c + 1) * BANK)
+                    p_acc = banks.tile([128, BANK], F32, name="p_acc")
+                    nc.tensor.matmul(p_acc[:], w_src_sb[:, rows], x_bf[:, cols], start=True, stop=True)
+                    nc.scalar.activation(window[:, cols], p_acc[:], COPY)
+
+                for piece in range(N // PIECE):
+                    q = pieces.tile([128, PIECE], F32, name="q")
+                    for c in range(PIECE // BANK):
+                        q_acc = banks.tile([128, BANK], F32, name="q_acc")
+                        first = piece * PIECE + c * BANK
+                        nc.tensor.matmul(
+                            q_acc[:], w_dst_sb[:, rows], d_bf[:, first : first + BANK], start=True, stop=True
+                        )
+                        nc.scalar.activation(
+                            q[:, c * BANK : (c + 1) * BANK], q_acc[:], IDENTITY, bias=bias[g][:]
+                        )
+
+                    total = pieces.tile([128, PIECE], F32, name="total")
+                    picked = window[:].indirect(offsets[:, piece * (PIECE // 16) : (piece + 1) * (PIECE // 16)])
+                    nc.vector.tensor_tensor(total[:], picked, q[:], ADD)
+                    first_row = t * M + g * 128
+                    nc.sync.dma_start(
+                        out[first_row : first_row + 128, piece * PIECE : (piece + 1) * PIECE], total[:]
+                    )

@@ -22,14 +22,23 @@ def tile_globallocalencoder_kernel(tc, x, dst, w_src, w_dst, b, offs, out):
     nc = tc.nc
     with (
         tc.tile_pool(name="held", bufs=1) as held,
-        tc.tile_pool(name="raw", bufs=T) as raw,
+        tc.tile_pool(name="raw", bufs=3) as raw,
         tc.tile_pool(name="rounded", bufs=2) as rounded,
         tc.tile_pool(name="windows", bufs=3) as windows,
-        tc.tile_pool(name="pieces", bufs=4) as pieces,
+        tc.tile_pool(name="addends", bufs=3) as addends,
+        tc.tile_pool(name="sums", bufs=6) as sums,
         tc.psum_pool(name="banks", bufs=4) as banks,
     ):
-        offsets = held.tile([128, N // 16], U16, name="offsets")
-        nc.sync.dma_start(offsets[:], offs)
+
+        def load(raw_tile, source, t, width):
+            for first in range(0, raw_tile.shape[1], width):
+                cols = slice(first, first + width)
+                nc.sync.dma_start(raw_tile[:, cols], source[t * H : (t + 1) * H, cols])
+
+        def round_to_bf16(engine, bf_tile, raw_tile, first, stop, width):
+            for start in range(first, stop, width):
+                cols = slice(start, start + width)
+                engine.tensor_copy(bf_tile[:, cols], raw_tile[:, cols])
 
         w_src_sb = held.tile([H, M], BF16, name="w_src_sb")
         w_dst_sb = held.tile([H, M], BF16, name="w_dst_sb")
@@ -39,51 +48,54 @@ def tile_globallocalencoder_kernel(tc, x, dst, w_src, w_dst, b, offs, out):
         for g in range(M // 128):
             nc.scalar.dma_start(bias[g][:], b[g * 128 : (g + 1) * 128, :])
 
-        x_raw = []
-        dst_raw = []
-        for t in range(T):
-            x_t = raw.tile([H, S], F32, name="x_t")
-            nc.sync.dma_start(x_t[:], x[t * H : (t + 1) * H, :])
-            d_t = raw.tile([H, N], F32, name="d_t")
-            for c in range(N // PIECE):
-                cols = slice(c * PIECE, (c + 1) * PIECE)
-                nc.sync.dma_start(d_t[:, cols], dst[t * H : (t + 1) * H, cols])
-            x_raw.append(x_t)
-            dst_raw.append(d_t)
+        x_raw = [raw.tile([H, S], F32, name="x_raw")]
+        d_raw = [raw.tile([H, N], F32, name="d_raw")]
+        load(x_raw[0], x, 0, BANK)
+        offsets = held.tile([128, N // 16], U16, name="offsets")
+        nc.sync.dma_start(offsets[:], offs)
+        load(d_raw[0], dst, 0, BANK)
 
         for t in range(T):
+            if t + 1 < T:
+                x_raw.append(raw.tile([H, S], F32, name="x_raw"))
+                d_raw.append(raw.tile([H, N], F32, name="d_raw"))
+                load(x_raw[t + 1], x, t + 1, PIECE)
+                load(d_raw[t + 1], dst, t + 1, PIECE)
+
             x_bf = rounded.tile([H, S], BF16, name="x_bf")
-            nc.gpsimd.tensor_copy(x_bf[:], x_raw[t][:])
             d_bf = rounded.tile([H, N], BF16, name="d_bf")
-            for c in range(N // PIECE):
-                cols = slice(c * PIECE, (c + 1) * PIECE)
-                nc.gpsimd.tensor_copy(d_bf[:, cols], dst_raw[t][:, cols])
+            if t == 0:
+                round_to_bf16(nc.vector, x_bf, x_raw[t], 0, S, BANK)
+                round_to_bf16(nc.vector, d_bf, d_raw[t], 0, PIECE, BANK)
+                round_to_bf16(nc.gpsimd, d_bf, d_raw[t], PIECE, N, BANK)
+            else:
+                round_to_bf16(nc.gpsimd, x_bf, x_raw[t], 0, S, PIECE)
+                round_to_bf16(nc.gpsimd, d_bf, d_raw[t], 0, N, PIECE)
 
             for g in range(M // 128):
                 rows = slice(g * 128, (g + 1) * 128)
                 window = windows.tile([128, S], F32, name="window")
-                for c in range(S // BANK):
-                    cols = slice(c * BANK, (c + 1) * BANK)
+                for first in range(0, S, BANK):
+                    cols = slice(first, first + BANK)
                     p_acc = banks.tile([128, BANK], F32, name="p_acc")
                     nc.tensor.matmul(p_acc[:], w_src_sb[:, rows], x_bf[:, cols], start=True, stop=True)
                     nc.scalar.activation(window[:, cols], p_acc[:], COPY)
 
-                for piece in range(N // PIECE):
-                    q = pieces.tile([128, PIECE], F32, name="q")
-                    for c in range(PIECE // BANK):
+                for piece in range(0, N, PIECE):
+                    q = addends.tile([128, PIECE], F32, name="q")
+                    for first in range(0, PIECE, BANK):
                         q_acc = banks.tile([128, BANK], F32, name="q_acc")
-                        first = piece * PIECE + c * BANK
                         nc.tensor.matmul(
-                            q_acc[:], w_dst_sb[:, rows], d_bf[:, first : first + BANK], start=True, stop=True
+                            q_acc[:],
+                            w_dst_sb[:, rows],
+                            d_bf[:, piece + first : piece + first + BANK],
+                            start=True,
+                            stop=True,
                         )
-                        nc.scalar.activation(
-                            q[:, c * BANK : (c + 1) * BANK], q_acc[:], IDENTITY, bias=bias[g][:]
-                        )
+                        nc.scalar.activation(q[:, first : first + BANK], q_acc[:], IDENTITY, bias=bias[g][:])
 
-                    total = pieces.tile([128, PIECE], F32, name="total")
-                    picked = window[:].indirect(offsets[:, piece * (PIECE // 16) : (piece + 1) * (PIECE // 16)])
+                    total = sums.tile([128, PIECE], F32, name="total")
+                    picked = window[:].indirect(offsets[:, piece // 16 : (piece + PIECE) // 16])
                     nc.vector.tensor_tensor(total[:], picked, q[:], ADD)
                     first_row = t * M + g * 128
-                    nc.sync.dma_start(
-                        out[first_row : first_row + 128, piece * PIECE : (piece + 1) * PIECE], total[:]
-                    )
+                    nc.sync.dma_start(out[first_row : first_row + 128, piece : piece + PIECE], total[:])

@@ -22,10 +22,10 @@ def tile_globallocalencoder_kernel(tc, x, dst, w_src, w_dst, b, offs, out):
     nc = tc.nc
     with (
         tc.tile_pool(name="held", bufs=1) as held,
-        tc.tile_pool(name="raw", bufs=3) as raw,
+        tc.tile_pool(name="raw", bufs=T) as raw,
         tc.tile_pool(name="rounded", bufs=2) as rounded,
         tc.tile_pool(name="windows", bufs=3) as windows,
-        tc.tile_pool(name="addends", bufs=3) as addends,
+        tc.tile_pool(name="addends", bufs=4) as addends,
         tc.tile_pool(name="sums", bufs=6) as sums,
         tc.psum_pool(name="banks", bufs=4) as banks,
     ):
@@ -35,10 +35,10 @@ def tile_globallocalencoder_kernel(tc, x, dst, w_src, w_dst, b, offs, out):
                 cols = slice(first, first + width)
                 nc.sync.dma_start(raw_tile[:, cols], source[t * H : (t + 1) * H, cols])
 
-        def round_to_bf16(engine, bf_tile, raw_tile, first, stop, width):
+        def round_to_bf16(engine_copy, bf_tile, raw_tile, first, stop, width):
             for start in range(first, stop, width):
                 cols = slice(start, start + width)
-                engine.tensor_copy(bf_tile[:, cols], raw_tile[:, cols])
+                engine_copy(bf_tile[:, cols], raw_tile[:, cols])
 
         w_src_sb = held.tile([H, M], BF16, name="w_src_sb")
         w_dst_sb = held.tile([H, M], BF16, name="w_dst_sb")
@@ -48,32 +48,27 @@ def tile_globallocalencoder_kernel(tc, x, dst, w_src, w_dst, b, offs, out):
         for g in range(M // 128):
             nc.scalar.dma_start(bias[g][:], b[g * 128 : (g + 1) * 128, :])
 
-        x_raw = [raw.tile([H, S], F32, name="x_raw")]
-        d_raw = [raw.tile([H, N], F32, name="d_raw")]
+        x_raw = [raw.tile([H, S], F32, name="x_raw") for t in range(T)]
+        d_raw = [raw.tile([H, N], F32, name="d_raw") for t in range(T)]
         load(x_raw[0], x, 0, BANK)
         offsets = held.tile([128, N // 16], U16, name="offsets")
         nc.sync.dma_start(offsets[:], offs)
         load(d_raw[0], dst, 0, BANK)
+        for t in range(1, T):
+            load(x_raw[t], x, t, PIECE)
+            load(d_raw[t], dst, t, PIECE)
+
+        x_bf = rounded.tile([H, S], BF16, name="x_bf")
+        round_to_bf16(nc.vector.tensor_copy, x_bf, x_raw[0], 0, S, BANK)
 
         for t in range(T):
-            if t + 1 < T:
-                x_raw.append(raw.tile([H, S], F32, name="x_raw"))
-                d_raw.append(raw.tile([H, N], F32, name="d_raw"))
-                load(x_raw[t + 1], x, t + 1, PIECE)
-                load(d_raw[t + 1], dst, t + 1, PIECE)
-
-            x_bf = rounded.tile([H, S], BF16, name="x_bf")
             d_bf = rounded.tile([H, N], BF16, name="d_bf")
-            if t == 0:
-                round_to_bf16(nc.vector, x_bf, x_raw[t], 0, S, BANK)
-                round_to_bf16(nc.vector, d_bf, d_raw[t], 0, PIECE, BANK)
-                round_to_bf16(nc.gpsimd, d_bf, d_raw[t], PIECE, N, BANK)
-            else:
-                round_to_bf16(nc.gpsimd, x_bf, x_raw[t], 0, S, PIECE)
-                round_to_bf16(nc.gpsimd, d_bf, d_raw[t], 0, N, PIECE)
-
             for g in range(M // 128):
                 rows = slice(g * 128, (g + 1) * 128)
+                if g == 1 and t + 1 < T:
+                    next_x_bf = rounded.tile([H, S], BF16, name="x_bf")
+                    round_to_bf16(nc.vector.tensor_copy, next_x_bf, x_raw[t + 1], 0, S, S)
+
                 window = windows.tile([128, S], F32, name="window")
                 for first in range(0, S, BANK):
                     cols = slice(first, first + BANK)
@@ -82,6 +77,11 @@ def tile_globallocalencoder_kernel(tc, x, dst, w_src, w_dst, b, offs, out):
                     nc.scalar.activation(window[:, cols], p_acc[:], COPY)
 
                 for piece in range(0, N, PIECE):
+                    if t == 0 and g == 0 and piece == 0:
+                        round_to_bf16(nc.vector.tensor_copy, d_bf, d_raw[t], piece, piece + PIECE, BANK)
+                    elif g == 0:
+                        round_to_bf16(nc.scalar.copy, d_bf, d_raw[t], piece, piece + PIECE, PIECE)
+
                     q = addends.tile([128, PIECE], F32, name="q")
                     for first in range(0, PIECE, BANK):
                         q_acc = banks.tile([128, BANK], F32, name="q_acc")
@@ -99,3 +99,5 @@ def tile_globallocalencoder_kernel(tc, x, dst, w_src, w_dst, b, offs, out):
                     nc.vector.tensor_tensor(total[:], picked, q[:], ADD)
                     first_row = t * M + g * 128
                     nc.sync.dma_start(out[first_row : first_row + 128, piece : piece + PIECE], total[:])
+            if t + 1 < T:
+                x_bf = next_x_bf

@@ -14,8 +14,22 @@ S = 1024
 N = 2048
 BANK = 512
 PIECE = 1024
+SHORT = (256, 256, 512)
 
 FLOPS = 2 * T * H * M * (S + N)
+
+
+def cut(t, g, piece):
+    widths = [PIECE]
+    if (t, g, piece) == (0, 0, 0):
+        widths = list(SHORT)
+    if (t, g, piece) == (T - 1, M // 128 - 1, N // PIECE - 1):
+        widths = list(reversed(SHORT))
+    return [(piece * PIECE + sum(widths[:i]), width) for i, width in enumerate(widths)]
+
+
+def chunks(first, width, step):
+    return [(start, min(step, first + width - start)) for start in range(first, first + width, step)]
 
 
 def tile_globallocalencoder_kernel(tc, x, dst, w_src, w_dst, b, offs, out):
@@ -24,80 +38,93 @@ def tile_globallocalencoder_kernel(tc, x, dst, w_src, w_dst, b, offs, out):
         tc.tile_pool(name="held", bufs=1) as held,
         tc.tile_pool(name="raw", bufs=T) as raw,
         tc.tile_pool(name="rounded", bufs=2) as rounded,
-        tc.tile_pool(name="windows", bufs=3) as windows,
+        tc.tile_pool(name="windows", bufs=4) as windows,
         tc.tile_pool(name="addends", bufs=4) as addends,
         tc.tile_pool(name="sums", bufs=6) as sums,
         tc.psum_pool(name="banks", bufs=4) as banks,
     ):
-
-        def load(raw_tile, source, t, width):
-            for first in range(0, raw_tile.shape[1], width):
-                cols = slice(first, first + width)
-                nc.sync.dma_start(raw_tile[:, cols], source[t * H : (t + 1) * H, cols])
-
-        def round_to_bf16(engine_copy, bf_tile, raw_tile, first, stop, width):
-            for start in range(first, stop, width):
-                cols = slice(start, start + width)
-                engine_copy(bf_tile[:, cols], raw_tile[:, cols])
-
         w_src_sb = held.tile([H, M], BF16, name="w_src_sb")
         w_dst_sb = held.tile([H, M], BF16, name="w_dst_sb")
-        nc.scalar.dma_start(w_src_sb[:], w_src)
-        nc.scalar.dma_start(w_dst_sb[:], w_dst)
-        bias = [held.tile([128, 1], F32, name=f"bias{g}") for g in range(M // 128)]
-        for g in range(M // 128):
-            nc.scalar.dma_start(bias[g][:], b[g * 128 : (g + 1) * 128, :])
+        bias = held.tile([128, M // 128], F32, name="bias")
+        offsets = held.tile([128, N // 16], U16, name="offsets")
 
         x_raw = [raw.tile([H, S], F32, name="x_raw") for t in range(T)]
         d_raw = [raw.tile([H, N], F32, name="d_raw") for t in range(T)]
-        load(x_raw[0], x, 0, BANK)
-        offsets = held.tile([128, N // 16], U16, name="offsets")
+        nc.scalar.dma_start(w_src_sb[:], w_src)
+        nc.sync.dma_start(x_raw[0][:, :BANK], x[0:H, :BANK])
+        nc.scalar.dma_start(x_raw[0][:, BANK:], x[0:H, BANK:])
+        nc.sync.dma_start(d_raw[0][:, :BANK], dst[0:H, :BANK])
+        nc.scalar.dma_start(w_dst_sb[:], w_dst)
         nc.sync.dma_start(offsets[:], offs)
-        load(d_raw[0], dst, 0, BANK)
+        with nc.allow_non_contiguous_dma(reason="256 bias values, one to a partition and block"):
+            nc.scalar.dma_start(bias[:], b.rearrange("(g p) one -> p (g one)", p=128))
+        nc.sync.dma_start(d_raw[0][:, BANK:PIECE], dst[0:H, BANK:PIECE])
+        nc.sync.dma_start(d_raw[0][:, PIECE:], dst[0:H, PIECE:])
         for t in range(1, T):
-            load(x_raw[t], x, t, PIECE)
-            load(d_raw[t], dst, t, PIECE)
+            nc.sync.dma_start(x_raw[t][:], x[t * H : (t + 1) * H, :])
+            for start, size in chunks(0, N, PIECE):
+                nc.sync.dma_start(d_raw[t][:, start : start + size], dst[t * H : (t + 1) * H, start : start + size])
 
-        x_bf = rounded.tile([H, S], BF16, name="x_bf")
-        round_to_bf16(nc.vector.tensor_copy, x_bf, x_raw[0], 0, S, BANK)
+        x_bf = {}
+        d_bf = {}
+        window = {}
+        q = {}
 
-        for t in range(T):
-            d_bf = rounded.tile([H, N], BF16, name="d_bf")
-            for g in range(M // 128):
-                rows = slice(g * 128, (g + 1) * 128)
-                if g == 1 and t + 1 < T:
-                    next_x_bf = rounded.tile([H, S], BF16, name="x_bf")
-                    round_to_bf16(nc.vector.tensor_copy, next_x_bf, x_raw[t + 1], 0, S, S)
+        def round_inputs(t, g, first, width):
+            if g > 0:
+                return
+            if first == 0:
+                x_bf[t] = rounded.tile([H, S], BF16, name="x_bf")
+                d_bf[t] = rounded.tile([H, N], BF16, name="d_bf")
+            if t == 0:
+                if first == 0:
+                    for start, size in chunks(0, S, SHORT[0]):
+                        nc.vector.tensor_copy(x_bf[t][:, start : start + size], x_raw[t][:, start : start + size])
+                for start, size in chunks(first, width, BANK):
+                    nc.vector.tensor_copy(d_bf[t][:, start : start + size], d_raw[t][:, start : start + size])
+            else:
+                if first == 0:
+                    nc.vector.tensor_copy(x_bf[t][:], x_raw[t][:])
+                nc.scalar.copy(d_bf[t][:, first : first + width], d_raw[t][:, first : first + width])
 
-                window = windows.tile([128, S], F32, name="window")
-                for first in range(0, S, BANK):
-                    cols = slice(first, first + BANK)
+        def project(t, g, first, width):
+            rows = slice(g * 128, (g + 1) * 128)
+            if first == 0:
+                window[t, g] = windows.tile([128, S], F32, name="window")
+                for start, size in chunks(0, S, SHORT[0] if (t, g) == (0, 0) else BANK):
                     p_acc = banks.tile([128, BANK], F32, name="p_acc")
-                    nc.tensor.matmul(p_acc[:], w_src_sb[:, rows], x_bf[:, cols], start=True, stop=True)
-                    nc.scalar.activation(window[:, cols], p_acc[:], COPY)
+                    nc.tensor.matmul(
+                        p_acc[:, :size], w_src_sb[:, rows], x_bf[t][:, start : start + size], start=True, stop=True
+                    )
+                    nc.scalar.activation(window[t, g][:, start : start + size], p_acc[:, :size], COPY)
+            q[t, g, first] = addends.tile([128, PIECE], F32, name="q")
+            for start, size in chunks(first, width, BANK):
+                q_acc = banks.tile([128, BANK], F32, name="q_acc")
+                nc.tensor.matmul(
+                    q_acc[:, :size], w_dst_sb[:, rows], d_bf[t][:, start : start + size], start=True, stop=True
+                )
+                nc.scalar.activation(
+                    q[t, g, first][:, start - first : start - first + size], q_acc[:, :size], IDENTITY, bias=bias[:, g : g + 1]
+                )
 
-                for piece in range(0, N, PIECE):
-                    if t == 0 and g == 0 and piece == 0:
-                        round_to_bf16(nc.vector.tensor_copy, d_bf, d_raw[t], piece, piece + PIECE, BANK)
-                    elif g == 0:
-                        round_to_bf16(nc.scalar.copy, d_bf, d_raw[t], piece, piece + PIECE, PIECE)
+        def gather_add(t, g, first, width):
+            total = sums.tile([128, PIECE], F32, name="total")
+            picked = window[t, g][:].indirect(offsets[:, first // 16 : (first + width) // 16])
+            nc.vector.tensor_tensor(total[:, :width], picked, q[t, g, first][:, :width], ADD)
+            first_row = t * M + g * 128
+            nc.sync.dma_start(out[first_row : first_row + 128, first : first + width], total[:, :width])
 
-                    q = addends.tile([128, PIECE], F32, name="q")
-                    for first in range(0, PIECE, BANK):
-                        q_acc = banks.tile([128, BANK], F32, name="q_acc")
-                        nc.tensor.matmul(
-                            q_acc[:],
-                            w_dst_sb[:, rows],
-                            d_bf[:, piece + first : piece + first + BANK],
-                            start=True,
-                            stop=True,
-                        )
-                        nc.scalar.activation(q[:, first : first + BANK], q_acc[:], IDENTITY, bias=bias[g][:])
-
-                    total = sums.tile([128, PIECE], F32, name="total")
-                    picked = window[:].indirect(offsets[:, piece // 16 : (piece + PIECE) // 16])
-                    nc.vector.tensor_tensor(total[:], picked, q[:], ADD)
-                    first_row = t * M + g * 128
-                    nc.sync.dma_start(out[first_row : first_row + 128, piece : piece + PIECE], total[:])
-            if t + 1 < T:
-                x_bf = next_x_bf
+        units = [
+            (t, g, first, width)
+            for t in range(T)
+            for piece in range(N // PIECE)
+            for g in range(M // 128)
+            for first, width in cut(t, g, piece)
+        ]
+        for u in range(-2, len(units)):
+            if u + 2 < len(units):
+                round_inputs(*units[u + 2])
+            if 0 <= u + 1 < len(units):
+                project(*units[u + 1])
+            if u >= 0:
+                gather_add(*units[u])

@@ -12,9 +12,13 @@ H = 128
 M = 256
 S = 1024
 N = 2048
+ROWS = 128
+BLOCKS = M // ROWS
 BANK = 512
 PIECE = 1024
-SHORT = (256, 256, 512)
+PIECES = N // PIECE
+SMALL = 256
+SHORT = (SMALL, SMALL, 2 * SMALL)
 
 FLOPS = 2 * T * H * M * (S + N)
 
@@ -23,7 +27,7 @@ def cut(t, g, piece):
     widths = [PIECE]
     if (t, g, piece) == (0, 0, 0):
         widths = list(SHORT)
-    if (t, g, piece) == (T - 1, M // 128 - 1, N // PIECE - 1):
+    if (t, g, piece) == (T - 1, BLOCKS - 1, PIECES - 1):
         widths = list(reversed(SHORT))
     return [(piece * PIECE + sum(widths[:i]), width) for i, width in enumerate(widths)]
 
@@ -38,18 +42,18 @@ def tile_globallocalencoder_kernel(tc, x, dst, w_src, w_dst, b, offs, out):
         tc.tile_pool(name="held", bufs=1) as held,
         tc.tile_pool(name="raw", bufs=T) as raw,
         tc.tile_pool(name="rounded", bufs=2) as rounded,
-        tc.tile_pool(name="windows", bufs=4) as windows,
-        tc.tile_pool(name="addends", bufs=4) as addends,
+        tc.tile_pool(name="windows", bufs=2 * BLOCKS) as windows,
+        tc.tile_pool(name="addends", bufs=6) as addends,
         tc.tile_pool(name="sums", bufs=6) as sums,
         tc.psum_pool(name="banks", bufs=4) as banks,
     ):
         w_src_sb = held.tile([H, M], BF16, name="w_src_sb")
         w_dst_sb = held.tile([H, M], BF16, name="w_dst_sb")
-        bias = held.tile([128, M // 128], F32, name="bias")
+        bias = held.tile([ROWS, BLOCKS], F32, name="bias")
         offsets = held.tile([128, N // 16], U16, name="offsets")
-
         x_raw = [raw.tile([H, S], F32, name="x_raw") for t in range(T)]
         d_raw = [raw.tile([H, N], F32, name="d_raw") for t in range(T)]
+
         nc.scalar.dma_start(w_src_sb[:], w_src)
         nc.sync.dma_start(x_raw[0][:, :BANK], x[0:H, :BANK])
         nc.scalar.dma_start(x_raw[0][:, BANK:], x[0:H, BANK:])
@@ -57,7 +61,7 @@ def tile_globallocalencoder_kernel(tc, x, dst, w_src, w_dst, b, offs, out):
         nc.scalar.dma_start(w_dst_sb[:], w_dst)
         nc.sync.dma_start(offsets[:], offs)
         with nc.allow_non_contiguous_dma(reason="256 bias values, one to a partition and block"):
-            nc.scalar.dma_start(bias[:], b.rearrange("(g p) one -> p (g one)", p=128))
+            nc.scalar.dma_start(bias[:], b.rearrange("(g p) one -> p (g one)", p=ROWS))
         nc.sync.dma_start(d_raw[0][:, BANK:PIECE], dst[0:H, BANK:PIECE])
         nc.sync.dma_start(d_raw[0][:, PIECE:], dst[0:H, PIECE:])
         for t in range(1, T):
@@ -76,49 +80,54 @@ def tile_globallocalencoder_kernel(tc, x, dst, w_src, w_dst, b, offs, out):
             if first == 0:
                 x_bf[t] = rounded.tile([H, S], BF16, name="x_bf")
                 d_bf[t] = rounded.tile([H, N], BF16, name="d_bf")
-            if t == 0:
-                if first == 0:
-                    for start, size in chunks(0, S, SHORT[0]):
+                if t == 0:
+                    for start, size in chunks(0, S, SMALL):
                         nc.vector.tensor_copy(x_bf[t][:, start : start + size], x_raw[t][:, start : start + size])
+                elif t < T - 1:
+                    nc.vector.tensor_copy(x_bf[t][:], x_raw[t][:])
+                else:
+                    nc.scalar.copy(x_bf[t][:], x_raw[t][:])
+            if t == 0:
                 for start, size in chunks(first, width, BANK):
                     nc.vector.tensor_copy(d_bf[t][:, start : start + size], d_raw[t][:, start : start + size])
             else:
-                if first == 0:
-                    nc.vector.tensor_copy(x_bf[t][:], x_raw[t][:])
                 nc.scalar.copy(d_bf[t][:, first : first + width], d_raw[t][:, first : first + width])
 
         def project(t, g, first, width):
-            rows = slice(g * 128, (g + 1) * 128)
+            rows = slice(g * ROWS, (g + 1) * ROWS)
             if first == 0:
-                window[t, g] = windows.tile([128, S], F32, name="window")
-                for start, size in chunks(0, S, SHORT[0] if (t, g) == (0, 0) else BANK):
-                    p_acc = banks.tile([128, BANK], F32, name="p_acc")
+                window[t, g] = windows.tile([ROWS, S], F32, name="window")
+                for start, size in chunks(0, S, SMALL if (t, g) == (0, 0) else BANK):
+                    p_acc = banks.tile([ROWS, BANK], F32, name="p_acc")
                     nc.tensor.matmul(
                         p_acc[:, :size], w_src_sb[:, rows], x_bf[t][:, start : start + size], start=True, stop=True
                     )
                     nc.scalar.activation(window[t, g][:, start : start + size], p_acc[:, :size], COPY)
-            q[t, g, first] = addends.tile([128, PIECE], F32, name="q")
+            q[t, g, first] = addends.tile([ROWS, PIECE], F32, name="q")
             for start, size in chunks(first, width, BANK):
-                q_acc = banks.tile([128, BANK], F32, name="q_acc")
+                q_acc = banks.tile([ROWS, BANK], F32, name="q_acc")
                 nc.tensor.matmul(
                     q_acc[:, :size], w_dst_sb[:, rows], d_bf[t][:, start : start + size], start=True, stop=True
                 )
                 nc.scalar.activation(
-                    q[t, g, first][:, start - first : start - first + size], q_acc[:, :size], IDENTITY, bias=bias[:, g : g + 1]
+                    q[t, g, first][:, start - first : start - first + size],
+                    q_acc[:, :size],
+                    IDENTITY,
+                    bias=bias[:, g : g + 1],
                 )
 
         def gather_add(t, g, first, width):
-            total = sums.tile([128, PIECE], F32, name="total")
+            total = sums.tile([ROWS, PIECE], F32, name="total")
             picked = window[t, g][:].indirect(offsets[:, first // 16 : (first + width) // 16])
             nc.vector.tensor_tensor(total[:, :width], picked, q[t, g, first][:, :width], ADD)
-            first_row = t * M + g * 128
-            nc.sync.dma_start(out[first_row : first_row + 128, first : first + width], total[:, :width])
+            first_row = t * M + g * ROWS
+            nc.sync.dma_start(out[first_row : first_row + ROWS, first : first + width], total[:, :width])
 
         units = [
             (t, g, first, width)
             for t in range(T)
-            for piece in range(N // PIECE)
-            for g in range(M // 128)
+            for piece in range(PIECES)
+            for g in range(BLOCKS)
             for first, width in cut(t, g, piece)
         ]
         for u in range(-2, len(units)):

@@ -83,10 +83,8 @@ def tile_globallocalencoder_kernel(tc, x, dst, w_src, w_dst, b, offs, out):
                 if t == 0:
                     for start, size in chunks(0, S, SMALL):
                         nc.vector.tensor_copy(x_bf[t][:, start : start + size], x_raw[t][:, start : start + size])
-                elif t < T - 1:
-                    nc.vector.tensor_copy(x_bf[t][:], x_raw[t][:])
                 else:
-                    nc.scalar.copy(x_bf[t][:], x_raw[t][:])
+                    nc.vector.tensor_copy(x_bf[t][:], x_raw[t][:])
             if t == 0:
                 for start, size in chunks(first, width, BANK):
                     nc.vector.tensor_copy(d_bf[t][:, start : start + size], d_raw[t][:, start : start + size])

@@ -83,8 +83,10 @@ def tile_globallocalencoder_kernel(tc, x, dst, w_src, w_dst, b, offs, out):
                 if t == 0:
                     for start, size in chunks(0, S, SMALL):
                         nc.vector.tensor_copy(x_bf[t][:, start : start + size], x_raw[t][:, start : start + size])
-                else:
+                elif t == 1:
                     nc.vector.tensor_copy(x_bf[t][:], x_raw[t][:])
+                else:
+                    nc.scalar.copy(x_bf[t][:], x_raw[t][:])
             if t == 0:
                 for start, size in chunks(first, width, BANK):
                     nc.vector.tensor_copy(d_bf[t][:, start : start + size], d_raw[t][:, start : start + size])

@@ -91,7 +91,8 @@ def tile_globallocalencoder_kernel(tc, x, dst, w_src, w_dst, b, offs, out):
                 for start, size in chunks(first, width, BANK):
                     nc.vector.tensor_copy(d_bf[t][:, start : start + size], d_raw[t][:, start : start + size])
             else:
-                nc.scalar.copy(d_bf[t][:, first : first + width], d_raw[t][:, first : first + width])
+                for start, size in chunks(first, width, BANK):
+                    nc.scalar.copy(d_bf[t][:, start : start + size], d_raw[t][:, start : start + size])
 
         def project(t, g, first, width):
             rows = slice(g * ROWS, (g + 1) * ROWS)
@@ -123,17 +124,21 @@ def tile_globallocalencoder_kernel(tc, x, dst, w_src, w_dst, b, offs, out):
             first_row = t * M + g * ROWS
             nc.sync.dma_start(out[first_row : first_row + ROWS, first : first + width], total[:, :width])
 
+        def order(t):
+            if t < T - 1:
+                return [(g, piece) for piece in range(PIECES) for g in range(BLOCKS)]
+            return [(g, piece) for g in range(BLOCKS) for piece in range(PIECES)]
+
         units = [
-            (t, g, first, width)
-            for t in range(T)
-            for piece in range(PIECES)
-            for g in range(BLOCKS)
-            for first, width in cut(t, g, piece)
+            (t, g, first, width) for t in range(T) for g, piece in order(t) for first, width in cut(t, g, piece)
         ]
         for u in range(-2, len(units)):
-            if u + 2 < len(units):
+            late = u + 2 < len(units) and units[u + 2][:3] == (T - 1, 0, PIECE)
+            if u + 2 < len(units) and not late:
                 round_inputs(*units[u + 2])
             if 0 <= u + 1 < len(units):
                 project(*units[u + 1])
+            if late:
+                round_inputs(*units[u + 2])
             if u >= 0:
                 gather_add(*units[u])

@@ -5,7 +5,6 @@ BF16 = mybir.dt.bfloat16
 U16 = mybir.dt.uint16
 ADD = mybir.AluOpType.add
 IDENTITY = mybir.ActivationFunctionType.Identity
-COPY = mybir.ActivationFunctionType.Copy
 
 T = 4
 H = 128
@@ -84,7 +83,8 @@ def tile_globallocalencoder_kernel(tc, x, dst, w_src, w_dst, b, offs, out):
                     for start, size in chunks(0, S, SMALL):
                         nc.vector.tensor_copy(x_bf[t][:, start : start + size], x_raw[t][:, start : start + size])
                 elif t == 1:
-                    nc.vector.tensor_copy(x_bf[t][:], x_raw[t][:])
+                    nc.vector.tensor_copy(x_bf[t][:, :BANK], x_raw[t][:, :BANK])
+                    nc.scalar.copy(x_bf[t][:, BANK:], x_raw[t][:, BANK:])
                 else:
                     nc.scalar.copy(x_bf[t][:], x_raw[t][:])
             if t == 0:
@@ -103,7 +103,7 @@ def tile_globallocalencoder_kernel(tc, x, dst, w_src, w_dst, b, offs, out):
                     nc.tensor.matmul(
                         p_acc[:, :size], w_src_sb[:, rows], x_bf[t][:, start : start + size], start=True, stop=True
                     )
-                    nc.scalar.activation(window[t, g][:, start : start + size], p_acc[:, :size], COPY)
+                    nc.scalar.copy(window[t, g][:, start : start + size], p_acc[:, :size])
             q[t, g, first] = addends.tile([ROWS, PIECE], F32, name="q")
             for start, size in chunks(first, width, BANK):
                 q_acc = banks.tile([ROWS, BANK], F32, name="q_acc")

@@ -57,10 +57,10 @@ def tile_globallocalencoder_kernel(tc, x, dst, w_src, w_dst, b, offs, out):
         nc.sync.dma_start(x_raw[0][:, :BANK], x[0:H, :BANK])
         nc.scalar.dma_start(x_raw[0][:, BANK:], x[0:H, BANK:])
         nc.sync.dma_start(d_raw[0][:, :BANK], dst[0:H, :BANK])
-        nc.scalar.dma_start(w_dst_sb[:], w_dst)
-        nc.sync.dma_start(offsets[:], offs)
+        nc.sync.dma_start(w_dst_sb[:], w_dst)
         with nc.allow_non_contiguous_dma(reason="256 bias values, one to a partition and block"):
-            nc.scalar.dma_start(bias[:], b.rearrange("(g p) one -> p (g one)", p=ROWS))
+            nc.sync.dma_start(bias[:], b.rearrange("(g p) one -> p (g one)", p=ROWS))
+        nc.sync.dma_start(offsets[:], offs)
         nc.sync.dma_start(d_raw[0][:, BANK:PIECE], dst[0:H, BANK:PIECE])
         nc.sync.dma_start(d_raw[0][:, PIECE:], dst[0:H, PIECE:])
         for t in range(1, T):

@@ -91,7 +91,7 @@ def tile_globallocalencoder_kernel(tc, x, dst, w_src, w_dst, b, offs, out):
                 for start, size in chunks(first, width, BANK):
                     nc.vector.tensor_copy(d_bf[t][:, start : start + size], d_raw[t][:, start : start + size])
             else:
-                for start, size in chunks(first, width, BANK):
+                for start, size in chunks(first, width, BANK if t == T - 1 else PIECE):
                     nc.scalar.copy(d_bf[t][:, start : start + size], d_raw[t][:, start : start + size])
 
         def project(t, g, first, width):

import concourse.mybir as mybir

F32 = mybir.dt.float32
BF16 = mybir.dt.bfloat16
U16 = mybir.dt.uint16
ADD = mybir.AluOpType.add
IDENTITY = mybir.ActivationFunctionType.Identity

T = 4
H = 128
M = 256
S = 1024
N = 2048
ROWS = 128
BLOCKS = M // ROWS
BANK = 512
PIECE = 1024
PIECES = N // PIECE
SMALL = 256
SHORT = (SMALL, SMALL, 2 * SMALL)

FLOPS = 2 * T * H * M * (S + N)


def cut(t, g, piece):
    widths = [PIECE]
    if (t, g, piece) == (0, 0, 0):
        widths = list(SHORT)
    if (t, g, piece) == (T - 1, BLOCKS - 1, PIECES - 1):
        widths = list(reversed(SHORT))
    return [(piece * PIECE + sum(widths[:i]), width) for i, width in enumerate(widths)]


def chunks(first, width, step):
    return [(start, min(step, first + width - start)) for start in range(first, first + width, step)]


def tile_globallocalencoder_kernel(tc, x, dst, w_src, w_dst, b, offs, out):
    nc = tc.nc
    with (
        tc.tile_pool(name="held", bufs=1) as held,
        tc.tile_pool(name="raw", bufs=T) as raw,
        tc.tile_pool(name="rounded", bufs=2) as rounded,
        tc.tile_pool(name="windows", bufs=2 * BLOCKS) as windows,
        tc.tile_pool(name="addends", bufs=6) as addends,
        tc.tile_pool(name="sums", bufs=6) as sums,
        tc.psum_pool(name="banks", bufs=4) as banks,
    ):
        w_src_sb = held.tile([H, M], BF16, name="w_src_sb")
        w_dst_sb = held.tile([H, M], BF16, name="w_dst_sb")
        bias = held.tile([ROWS, BLOCKS], F32, name="bias")
        offsets = held.tile([128, N // 16], U16, name="offsets")
        x_raw = [raw.tile([H, S], F32, name="x_raw") for t in range(T)]
        d_raw = [raw.tile([H, N], F32, name="d_raw") for t in range(T)]

        nc.scalar.dma_start(w_src_sb[:], w_src)
        nc.sync.dma_start(x_raw[0][:, :BANK], x[0:H, :BANK])
        nc.scalar.dma_start(x_raw[0][:, BANK:], x[0:H, BANK:])
        nc.sync.dma_start(d_raw[0][:, :BANK], dst[0:H, :BANK])
        nc.sync.dma_start(w_dst_sb[:], w_dst)
        with nc.allow_non_contiguous_dma(reason="256 bias values, one to a partition and block"):
            nc.sync.dma_start(bias[:], b.rearrange("(g p) one -> p (g one)", p=ROWS))
        nc.sync.dma_start(offsets[:], offs)
        nc.sync.dma_start(d_raw[0][:, BANK:PIECE], dst[0:H, BANK:PIECE])
        nc.sync.dma_start(d_raw[0][:, PIECE:], dst[0:H, PIECE:])
        for t in range(1, T):
            nc.sync.dma_start(x_raw[t][:], x[t * H : (t + 1) * H, :])
            for start, size in chunks(0, N, PIECE):
                nc.sync.dma_start(d_raw[t][:, start : start + size], dst[t * H : (t + 1) * H, start : start + size])

        x_bf = {}
        d_bf = {}
        window = {}
        q = {}

        def round_inputs(t, g, first, width):
            if g > 0:
                return
            if first == 0:
                x_bf[t] = rounded.tile([H, S], BF16, name="x_bf")
                d_bf[t] = rounded.tile([H, N], BF16, name="d_bf")
                if t == 0:
                    for start, size in chunks(0, S, SMALL):
                        nc.vector.tensor_copy(x_bf[t][:, start : start + size], x_raw[t][:, start : start + size])
                elif t == 1:
                    nc.vector.tensor_copy(x_bf[t][:, :BANK], x_raw[t][:, :BANK])
                    nc.scalar.copy(x_bf[t][:, BANK:], x_raw[t][:, BANK:])
                else:
                    nc.scalar.copy(x_bf[t][:], x_raw[t][:])
            if t == 0:
                for start, size in chunks(first, width, BANK):
                    nc.vector.tensor_copy(d_bf[t][:, start : start + size], d_raw[t][:, start : start + size])
            else:
                for start, size in chunks(first, width, BANK if t == T - 1 else PIECE):
                    nc.scalar.copy(d_bf[t][:, start : start + size], d_raw[t][:, start : start + size])

        def project(t, g, first, width):
            rows = slice(g * ROWS, (g + 1) * ROWS)
            if first == 0:
                window[t, g] = windows.tile([ROWS, S], F32, name="window")
                for start, size in chunks(0, S, SMALL if (t, g) == (0, 0) else BANK):
                    p_acc = banks.tile([ROWS, BANK], F32, name="p_acc")
                    nc.tensor.matmul(
                        p_acc[:, :size], w_src_sb[:, rows], x_bf[t][:, start : start + size], start=True, stop=True
                    )
                    nc.scalar.copy(window[t, g][:, start : start + size], p_acc[:, :size])
            q[t, g, first] = addends.tile([ROWS, PIECE], F32, name="q")
            for start, size in chunks(first, width, BANK):
                q_acc = banks.tile([ROWS, BANK], F32, name="q_acc")
                nc.tensor.matmul(
                    q_acc[:, :size], w_dst_sb[:, rows], d_bf[t][:, start : start + size], start=True, stop=True
                )
                nc.scalar.activation(
                    q[t, g, first][:, start - first : start - first + size],
                    q_acc[:, :size],
                    IDENTITY,
                    bias=bias[:, g : g + 1],
                )

        def gather_add(t, g, first, width):
            total = sums.tile([ROWS, PIECE], F32, name="total")
            picked = window[t, g][:].indirect(offsets[:, first // 16 : (first + width) // 16])
            nc.vector.tensor_tensor(total[:, :width], picked, q[t, g, first][:, :width], ADD)
            first_row = t * M + g * ROWS
            nc.sync.dma_start(out[first_row : first_row + ROWS, first : first + width], total[:, :width])

        def order(t):
            if t < T - 1:
                return [(g, piece) for piece in range(PIECES) for g in range(BLOCKS)]
            return [(g, piece) for g in range(BLOCKS) for piece in range(PIECES)]

        units = [
            (t, g, first, width) for t in range(T) for g, piece in order(t) for first, width in cut(t, g, piece)
        ]
        for u in range(-2, len(units)):
            late = u + 2 < len(units) and units[u + 2][:3] == (T - 1, 0, PIECE)
            if u + 2 < len(units) and not late:
                round_inputs(*units[u + 2])
            if 0 <= u + 1 < len(units):
                project(*units[u + 1])
            if late:
                round_inputs(*units[u + 2])
            if u >= 0:
                gather_add(*units[u])
